import numpy as np
import ml_dtypes


def mxq(x, axis, fmt="e4m3"):
    dtype, down = {"e4m3": (ml_dtypes.float8_e4m3fn, 7), "e5m2": (ml_dtypes.float8_e5m2, 14)}[fmt]
    v = np.moveaxis(np.asarray(x, np.float32).astype(ml_dtypes.bfloat16).astype(np.float64), axis, -1)
    blocks = v.reshape(v.shape[:-1] + (-1, 32))
    amax = np.abs(blocks).max(-1, keepdims=True)
    byte = np.maximum(np.where(amax > 0, np.frexp(amax)[1] - 1 + 127, 0) - down, 1)
    scale = np.exp2(byte - 127.0)
    codes = (blocks / scale).astype(np.float32).astype(dtype).astype(np.float64)
    return np.moveaxis((codes * scale).reshape(v.shape), -1, axis)


WIDE = False


def mx_kscale(k):
    if not WIDE:
        return np.ones(k)
    levels = np.array([10, -10, 5, -5, 0])
    a = np.random.permutation(np.resize(levels, k // 512 * 4)).reshape(k // 512, 4)
    idx = np.arange(k)
    return np.exp2(a[idx // 512, idx % 128 // 32])


BF16 = ml_dtypes.bfloat16


def bf(x):
    return np.asarray(x, np.float32).astype(BF16)


def f64(x):
    return np.asarray(x).astype(np.float64)


B, K_SLOTS, P, SLOT, HID, NC, NP = 256, 8, 1536, 512, 512, 512, 512
KEY_SCALE = 3.0


def softmax(z):
    e = np.exp(z - z.max(-1, keepdims=True))
    return e / e.sum(-1, keepdims=True)


def setup_inputs():
    rn = np.random.standard_normal
    s, t = mx_kscale(P), mx_kscale(P)
    return {"inst_embed": bf(rn((B, P)) * s),
            "Wfc": bf(rn((P, P)) / np.sqrt(P) / s[:, None] * t), "bfc": bf(0.3 * rn(P) * t),
            "Wfp": bf(rn((P, P)) / np.sqrt(P) / s[:, None] * t), "bfp": bf(0.3 * rn(P) * t),
            "Kc": bf(KEY_SCALE * rn((NC, P)) / t), "Kp": bf(KEY_SCALE * rn((NP, P)) / t)}


def reference(inst_embed, Wfc, bfc, Wfp, bfp, Kc, Kp):
    xq = mxq(f64(inst_embed), 1, "e4m3")
    Qc = (xq @ mxq(f64(Wfc), 0, "e4m3")) + f64(bfc)
    Qp = (xq @ mxq(f64(Wfp), 0, "e4m3")) + f64(bfp)
    zc = (mxq(Qc, 1, "e4m3") @ mxq(f64(Kc), 1, "e4m3").T) / np.sqrt(P)
    zp = (mxq(Qp, 1, "e4m3") @ mxq(f64(Kp), 1, "e4m3").T) / np.sqrt(P)
    return softmax(zc), softmax(zp)

@@ -1,0 +1,365 @@
+from contextlib import ExitStack
+import math
+
+import concourse.mybir as mybir
+from concourse.masks import make_identity
+
+BF16 = mybir.dt.bfloat16
+F32 = mybir.dt.float32
+U32 = mybir.dt.uint32
+U8 = mybir.dt.uint8
+FP8X4 = mybir.dt.float8_e4m3fn_x4
+ADD = mybir.AluOpType.add
+EXP = mybir.ActivationFunctionType.Exp
+COPY = mybir.ActivationFunctionType.Copy
+
+P = 128
+PACK = 4
+K_PASS = P * PACK
+HALF_PASS = K_PASS // 2
+PASS_WORDS = K_PASS // 2
+
+BATCH = 256
+DIM = 1536
+CODES = 512
+PASSES = DIM // K_PASS
+BATCH_TILES = BATCH // P
+KEY_TILES = CODES // P
+WORDS = DIM // 2
+BRANCHES = 2
+
+FLOPS = BRANCHES * (2 * BATCH * DIM * DIM + 2 * BATCH * CODES * DIM)
+
+UNITS_PER_BRANCH = PASSES * PASSES
+N_UNITS = BRANCHES * UNITS_PER_BRANCH
+X_FIRST_STEP = 3
+KEY_FIRST_STEP = 9
+KEY_UNITS_PER_STEP = 2
+KEY_UNITS = (KEY_TILES // 2) * PASSES
+
+
+def tile_executor_pa_kernel(
+    tc, inst_embed, Wfc, bfc, Wfp, bfp, Kc, Kp, out_0, out_1
+):
+    nc = tc.nc
+    weights = (Wfc, Wfp)
+    biases = (bfc, bfp)
+    keys = (Kc, Kp)
+    outs = (out_0, out_1)
+    inv_sqrt_dim = 1.0 / math.sqrt(DIM)
+
+    with ExitStack() as ctx:
+        ctx.enter_context(tc.manual_schedule())
+        resident = ctx.enter_context(tc.tile_pool(name="resident", bufs=1))
+        w_stage = ctx.enter_context(tc.tile_pool(name="w_stage", bufs=6))
+        k_stage = ctx.enter_context(tc.tile_pool(name="k_stage", bufs=4))
+        q_stage = ctx.enter_context(tc.tile_pool(name="q_stage", bufs=4))
+        small = ctx.enter_context(tc.tile_pool(name="small", bufs=4))
+        banks = ctx.enter_context(tc.psum_pool(name="banks", bufs=6))
+        z_psum = ctx.enter_context(tc.psum_pool(name="z_psum", bufs=BATCH_TILES))
+
+        bias_rows = resident.tile([P, HALF_PASS], BF16)
+        nc.vector.memset(bias_rows[:], 0.0)
+        rows_per_bias = DIM // HALF_PASS
+        for br in range(BRANCHES):
+            nc.sync.dma_start(
+                out=bias_rows[br * rows_per_bias : (br + 1) * rows_per_bias, :],
+                in_=biases[br].rearrange("(r w) -> r w", w=HALF_PASS),
+            )
+
+        identity = resident.tile([P, P], F32)
+        make_identity(nc, identity[:])
+
+        exp_in = resident.tile([P, 1], F32)
+        exp_out = resident.tile([P, 1], F32)
+        nc.vector.memset(exp_in[:], 0.0)
+        nc.scalar.activation(out=exp_out[:], in_=exp_in[:], func=EXP)
+
+        w_raw = {}
+
+        def load_weights(br, c):
+            raw = resident.tile([P, PACK, DIM], BF16, name="w_raw_%d_%d" % (br, c))
+            for u in range(2):
+                first = K_PASS * c + HALF_PASS * u
+                nc.sync.dma_start(
+                    out=raw[:, 2 * u : 2 * u + 2, :],
+                    in_=weights[br][first : first + HALF_PASS, :].rearrange(
+                        "(q e) n -> q e n", e=2
+                    ),
+                )
+            w_raw[(br, c)] = raw
+
+        x_rows = resident.tile([P, BATCH_TILES * DIM], BF16)
+
+        def load_embedding():
+            nc.sync.dma_start(
+                out=x_rows[:], in_=inst_embed.rearrange("(p h) k -> p (h k)", h=BATCH_TILES)
+            )
+
+        key_rows = {}
+
+        def load_keys(br):
+            rows = resident.tile([P, KEY_TILES * DIM], BF16, name="key_rows_%d" % br)
+            for pair in range(KEY_TILES // 2):
+                nc.sync.dma_start(
+                    out=rows[:, 2 * pair * DIM : 2 * (pair + 1) * DIM].rearrange(
+                        "p (r k) -> p r k", r=2
+                    ),
+                    in_=keys[br][2 * pair * P : 2 * (pair + 1) * P, :].rearrange(
+                        "(r p) k -> p r k", p=P
+                    ),
+                )
+            key_rows[br] = rows
+
+        load_weights(0, 0)
+        load_weights(0, 1)
+        load_embedding()
+        load_weights(0, 2)
+        load_weights(1, 0)
+        load_keys(0)
+        load_weights(1, 1)
+        load_keys(1)
+        load_weights(1, 2)
+
+        def packed(name, width):
+            codes = resident.tile([P, width], U32, align_bytes=64, name="%s_codes" % name)
+            scales = resident.tile([P, width], U8, align_bytes=64, name="%s_scales" % name)
+            return codes, scales
+
+        x_packed = packed("x", PASSES * BATCH)
+        w_packed = [packed("w%d" % br, PASSES * DIM) for br in range(BRANCHES)]
+        q_packed = [packed("q%d" % br, PASSES * BATCH) for br in range(BRANCHES)]
+        k_packed = [packed("k%d" % br, PASSES * CODES) for br in range(BRANCHES)]
+
+        def quantise(grouped, operand, first, width):
+            codes, scales = operand
+            nc.vector.quantize_mx(
+                out=codes[:, first : first + width].bitcast(FP8X4),
+                scales=scales[:, first : first + width],
+                in_=grouped,
+            )
+
+        def multiply(out, stationary, s_first, moving, m_first, m_width, start, stop):
+            s_codes, s_scales = stationary
+            m_codes, m_scales = moving
+            nc.tensor.matmul_mx(
+                out=out,
+                lhsT=s_codes[:, s_first : s_first + P].bitcast(FP8X4),
+                lhsT_scale=s_scales[:, s_first : s_first + P],
+                rhs=m_codes[:, m_first : m_first + m_width].bitcast(FP8X4),
+                rhs_scale=m_scales[:, m_first : m_first + m_width],
+                start=start,
+                stop=stop,
+            )
+
+        bias_bank = banks.tile([P, 2, 2 * P], F32, name="bank")
+        nc.tensor.transpose(bias_bank[:, 0, 0:P], bias_rows[:].bitcast(F32), identity[:])
+        bias_words = BRANCHES * rows_per_bias
+        bias_pairs = resident.tile([P, 2 * bias_words], BF16)
+        bias_t = resident.tile([P, 2 * bias_words], F32)
+
+        def widen_biases():
+            nc.vector.tensor_copy(out=bias_pairs[:].bitcast(F32), in_=bias_bank[:, 0, 0:bias_words])
+            nc.vector.tensor_copy(out=bias_t[:], in_=bias_pairs[:])
+
+        w_grouped = {}
+
+        def regroup_weights(unit):
+            br, c, g = unit // UNITS_PER_BRANCH, (unit // PASSES) % PASSES, unit % PASSES
+            grouped = w_stage.tile([P, K_PASS * PACK], BF16, align_bytes=64, name="w_grouped")
+            for u in range(2):
+                first = K_PASS * g + HALF_PASS * u
+                src = w_raw[(br, c)][:, :, first : first + HALF_PASS].rearrange(
+                    "p t (q e) -> p q t e", e=2
+                )
+                dst = grouped[:, u * HALF_PASS * PACK : (u + 1) * HALF_PASS * PACK].rearrange(
+                    "p (e q t) -> p q t e", e=2, t=PACK
+                )
+                if u == 0:
+                    nc.vector.tensor_copy(out=dst, in_=src)
+                else:
+                    nc.scalar.copy(out=dst, in_=src)
+            w_grouped[unit] = grouped
+
+        def quantise_weights(unit):
+            br, c, g = unit // UNITS_PER_BRANCH, (unit // PASSES) % PASSES, unit % PASSES
+            quantise(w_grouped[unit][:], w_packed[br], c * DIM + g * K_PASS, K_PASS)
+
+        q_banks = {}
+
+        def project(br, g):
+            for h in range(BATCH_TILES):
+                bank = banks.tile([P, PACK, P], F32, name="bank")
+                for t in range(PACK):
+                    for c in range(PASSES):
+                        multiply(
+                            bank[:, t, :],
+                            w_packed[br],
+                            c * DIM + g * K_PASS + t * P,
+                            x_packed,
+                            c * BATCH + h * P,
+                            P,
+                            start=(c == 0),
+                            stop=(c == PASSES - 1),
+                        )
+                q_banks[(br, g, h)] = bank
+
+        def round_and_quantise_q(br, g):
+            first = (br * PASSES + g) * PACK
+            bias = bias_t[:, first : first + PACK].unsqueeze(1).to_broadcast([P, P, PACK])
+            rounded = []
+            for h in range(BATCH_TILES):
+                q_grouped = q_stage.tile([P, P, PACK], BF16, align_bytes=64)
+                nc.vector.tensor_tensor(
+                    out=q_grouped[:],
+                    in0=q_banks[(br, g, h)][:].rearrange("p t j -> p j t"),
+                    in1=bias,
+                    op=ADD,
+                )
+                rounded.append(q_grouped)
+            for h in range(BATCH_TILES):
+                quantise(
+                    rounded[h][:].rearrange("p j t -> p (j t)"),
+                    q_packed[br],
+                    g * BATCH + h * P,
+                    P,
+                )
+
+        pair_units = [(x_rows, 0, c, x_packed, c * BATCH) for c in range(PASSES)]
+        for br in range(BRANCHES):
+            for pair in range(KEY_TILES // 2):
+                for g in range(PASSES):
+                    pair_units.append(
+                        (key_rows[br], 2 * pair, g, k_packed[br], g * CODES + pair * 2 * P)
+                    )
+
+        def first_step(n):
+            if n < PASSES:
+                return X_FIRST_STEP + n
+            return KEY_FIRST_STEP + (n - PASSES) // KEY_UNITS_PER_STEP
+
+        def pair_units_begun_in(step):
+            return [n for n in range(len(pair_units)) if first_step(n) == step]
+
+        pair_banks = {}
+        pair_grouped = {}
+
+        def transpose_pairs(n):
+            rows, tile0, g = pair_units[n][0:3]
+            words = rows[:].bitcast(F32)
+            bank = banks.tile([P, 2, 2 * P], F32, name="bank")
+            for u in range(2):
+                for i in range(2):
+                    first = WORDS * (tile0 + i) + PASS_WORDS * g + P * u
+                    nc.tensor.transpose(
+                        bank[:, u, P * i : P * (i + 1)], words[:, first : first + P], identity[:]
+                    )
+            pair_banks[n] = bank
+
+        def interleave_pairs(n):
+            grouped = k_stage.tile([P, 2 * P * PACK], BF16, align_bytes=64, name="pair_grouped")
+            nc.scalar.copy(
+                out=grouped[:].bitcast(F32).rearrange("p (j u) -> p j u", u=2),
+                in_=pair_banks[n][:].rearrange("p u j -> p j u"),
+            )
+            pair_grouped[n] = grouped
+
+        def quantise_pairs(n):
+            operand, first = pair_units[n][3:5]
+            quantise(pair_grouped[n][:], operand, first, 2 * P)
+
+        def last_unit(br, g):
+            return br * UNITS_PER_BRANCH + (PASSES - 1) * PASSES + g
+
+        def score_step(br, g):
+            last_key_unit = PASSES + (br + 1) * KEY_UNITS - 1
+            return max(last_unit(br, g) + 2, first_step(last_key_unit) + 2)
+
+        scores = {}
+        shifts = {}
+        sums = {}
+        probs = {}
+
+        def score_pass(br, g):
+            for h in range(BATCH_TILES):
+                if g == 0:
+                    scores[(br, h)] = z_psum.tile([P, CODES], F32, name="scores")
+                multiply(
+                    scores[(br, h)][:],
+                    q_packed[br],
+                    g * BATCH + h * P,
+                    k_packed[br],
+                    g * CODES,
+                    CODES,
+                    start=(g == 0),
+                    stop=(g == PASSES - 1),
+                )
+
+        def row_maxima(br):
+            for h in range(BATCH_TILES):
+                row_max = small.tile([P, 1], F32)
+                nc.vector.reduce_max(
+                    out=row_max[:], in_=scores[(br, h)][:], axis=mybir.AxisListType.X
+                )
+                shift = small.tile([P, 1], F32)
+                nc.vector.tensor_scalar_mul(out=shift[:], in0=row_max[:], scalar1=-inv_sqrt_dim)
+                shifts[(br, h)] = shift
+
+        def exponentials(br):
+            probs[br] = resident.tile([P, BATCH_TILES, CODES], F32, name="probs_%d" % br)
+            for h in range(BATCH_TILES):
+                row_sum = small.tile([P, 1], F32)
+                nc.scalar.activation(
+                    out=probs[br][:, h, :],
+                    in_=scores[(br, h)][:],
+                    func=EXP,
+                    bias=shifts[(br, h)][:],
+                    scale=inv_sqrt_dim,
+                    accum_out=row_sum[:],
+                )
+                sums[(br, h)] = row_sum
+
+        def normalise_and_store(br):
+            out_view = outs[br].rearrange("(p h) n -> p h n", h=BATCH_TILES)
+            for h in range(BATCH_TILES):
+                inv_sum = small.tile([P, 1], F32)
+                nc.vector.reciprocal(out=inv_sum[:], in_=sums[(br, h)][:])
+                nc.scalar.activation(
+                    out=probs[br][:, h, :], in_=probs[br][:, h, :], func=COPY, scale=inv_sum[:]
+                )
+                nc.sync.dma_start(out=out_view[:, h, :], in_=probs[br][:, h, :])
+
+        last_step = score_step(BRANCHES - 1, PASSES - 1) + 3
+        for step in range(last_step + 1):
+            if step < N_UNITS:
+                regroup_weights(step)
+            if 0 <= step - 1 < N_UNITS:
+                quantise_weights(step - 1)
+            if step == X_FIRST_STEP:
+                widen_biases()
+            for br in range(BRANCHES):
+                for g in range(PASSES):
+                    if step == last_unit(br, g) + 2:
+                        round_and_quantise_q(br, g)
+            for n in pair_units_begun_in(step - 2):
+                quantise_pairs(n)
+            for n in pair_units_begun_in(step - 1):
+                interleave_pairs(n)
+            for br in range(BRANCHES):
+                for g in range(PASSES):
+                    if step == last_unit(br, g) + 1:
+                        project(br, g)
+            for br in range(BRANCHES):
+                for g in range(PASSES):
+                    if step == score_step(br, g):
+                        score_pass(br, g)
+            for n in pair_units_begun_in(step):
+                transpose_pairs(n)
+            for br in range(BRANCHES):
+                scored = score_step(br, PASSES - 1)
+                if step == scored + 1:
+                    row_maxima(br)
+                if step == scored + 2:
+                    exponentials(br)
+                if step == scored + 3:
+                    normalise_and_store(br)

@@ -16,7 +16,6 @@ COPY = mybir.ActivationFunctionType.Copy
 P = 128
 PACK = 4
 K_PASS = P * PACK
-HALF_PASS = K_PASS // 2
 PASS_WORDS = K_PASS // 2
 
 BATCH = 256
@@ -25,7 +24,7 @@ CODES = 512
 PASSES = DIM // K_PASS
 BATCH_TILES = BATCH // P
 KEY_TILES = CODES // P
-WORDS = DIM // 2
+ROW_WORDS = DIM // 2
 BRANCHES = 2
 
 FLOPS = BRANCHES * (2 * BATCH * DIM * DIM + 2 * BATCH * CODES * DIM)
@@ -33,9 +32,8 @@ FLOPS = BRANCHES * (2 * BATCH * DIM * DIM + 2 * BATCH * CODES * DIM)
 UNITS_PER_BRANCH = PASSES * PASSES
 N_UNITS = BRANCHES * UNITS_PER_BRANCH
 X_FIRST_STEP = 3
-KEY_FIRST_STEP = 9
-KEY_UNITS_PER_STEP = 2
-KEY_UNITS = (KEY_TILES // 2) * PASSES
+KEY_FIRST_STEP = 10
+VECTOR_SHARE = 64
 
 
 def tile_executor_pa_kernel(
@@ -52,20 +50,11 @@ def tile_executor_pa_kernel(
         ctx.enter_context(tc.manual_schedule())
         resident = ctx.enter_context(tc.tile_pool(name="resident", bufs=1))
         w_stage = ctx.enter_context(tc.tile_pool(name="w_stage", bufs=6))
-        k_stage = ctx.enter_context(tc.tile_pool(name="k_stage", bufs=4))
-        q_stage = ctx.enter_context(tc.tile_pool(name="q_stage", bufs=4))
+        r_stage = ctx.enter_context(tc.tile_pool(name="r_stage", bufs=3))
+        q_stage = ctx.enter_context(tc.tile_pool(name="q_stage", bufs=2))
         small = ctx.enter_context(tc.tile_pool(name="small", bufs=4))
         banks = ctx.enter_context(tc.psum_pool(name="banks", bufs=6))
         z_psum = ctx.enter_context(tc.psum_pool(name="z_psum", bufs=BATCH_TILES))
-
-        bias_rows = resident.tile([P, HALF_PASS], BF16)
-        nc.vector.memset(bias_rows[:], 0.0)
-        rows_per_bias = DIM // HALF_PASS
-        for br in range(BRANCHES):
-            nc.sync.dma_start(
-                out=bias_rows[br * rows_per_bias : (br + 1) * rows_per_bias, :],
-                in_=biases[br].rearrange("(r w) -> r w", w=HALF_PASS),
-            )
 
         identity = resident.tile([P, P], F32)
         make_identity(nc, identity[:])
@@ -75,19 +64,27 @@ def tile_executor_pa_kernel(
         nc.vector.memset(exp_in[:], 0.0)
         nc.scalar.activation(out=exp_out[:], in_=exp_in[:], func=EXP)
 
+        bias_rows = resident.tile([P, K_PASS], BF16)
+        nc.vector.memset(bias_rows[:], 0.0)
+
         w_raw = {}
 
         def load_weights(br, c):
             raw = resident.tile([P, PACK, DIM], BF16, name="w_raw_%d_%d" % (br, c))
-            for u in range(2):
-                first = K_PASS * c + HALF_PASS * u
-                nc.sync.dma_start(
-                    out=raw[:, 2 * u : 2 * u + 2, :],
-                    in_=weights[br][first : first + HALF_PASS, :].rearrange(
-                        "(q e) n -> q e n", e=2
-                    ),
-                )
+            nc.sync.dma_start(
+                out=raw[:],
+                in_=weights[br][K_PASS * c : K_PASS * (c + 1), :].rearrange(
+                    "(p t) n -> p t n", t=PACK
+                ),
+            )
             w_raw[(br, c)] = raw
+
+        def load_biases():
+            for br in range(BRANCHES):
+                nc.sync.dma_start(
+                    out=bias_rows[br * PASSES : (br + 1) * PASSES, :],
+                    in_=biases[br].rearrange("(g k) -> g k", k=K_PASS),
+                )
 
         x_rows = resident.tile([P, BATCH_TILES * DIM], BF16)
 
@@ -100,18 +97,14 @@ def tile_executor_pa_kernel(
 
         def load_keys(br):
             rows = resident.tile([P, KEY_TILES * DIM], BF16, name="key_rows_%d" % br)
-            for pair in range(KEY_TILES // 2):
-                nc.sync.dma_start(
-                    out=rows[:, 2 * pair * DIM : 2 * (pair + 1) * DIM].rearrange(
-                        "p (r k) -> p r k", r=2
-                    ),
-                    in_=keys[br][2 * pair * P : 2 * (pair + 1) * P, :].rearrange(
-                        "(r p) k -> p r k", p=P
-                    ),
-                )
+            nc.sync.dma_start(
+                out=rows[:].rearrange("p (r k) -> p r k", r=KEY_TILES),
+                in_=keys[br].rearrange("(r p) k -> p r k", p=P),
+            )
             key_rows[br] = rows
 
         load_weights(0, 0)
+        load_biases()
         load_weights(0, 1)
         load_embedding()
         load_weights(0, 2)
@@ -152,14 +145,70 @@ def tile_executor_pa_kernel(
                 stop=stop,
             )
 
+        def transpose_words(bank, rows, tiles, g):
+            words = rows[:].bitcast(F32)
+            for u in range(2):
+                for i in range(len(tiles)):
+                    first = ROW_WORDS * tiles[i] + PASS_WORDS * g
+                    nc.tensor.transpose(
+                        bank[:, u, P * i : P * (i + 1)],
+                        words[:, first + u : first + PASS_WORDS : 2],
+                        identity[:],
+                    )
+
+        row_units = [(x_rows, BATCH_TILES, c, x_packed) for c in range(PASSES)]
+        for br in range(BRANCHES):
+            for g in range(PASSES):
+                row_units.append((key_rows[br], KEY_TILES, g, k_packed[br]))
+
+        def first_step(n):
+            if n < PASSES:
+                return X_FIRST_STEP + n
+            return KEY_FIRST_STEP + n - PASSES
+
+        def row_units_begun_in(step):
+            return [n for n in range(len(row_units)) if first_step(n) == step]
+
+        row_banks = {}
+        row_grouped = {}
+
+        def transpose_rows(n):
+            rows, n_tiles, g = row_units[n][0:3]
+            row_banks[n] = []
+            for pair in range(n_tiles // 2):
+                bank = banks.tile([P, 2, 2 * P], F32, name="bank")
+                transpose_words(bank, rows, (2 * pair, 2 * pair + 1), g)
+                row_banks[n].append(bank)
+
+        def interleave_rows(n):
+            n_tiles = row_units[n][1]
+            grouped = r_stage.tile([P, KEY_TILES * P * PACK], BF16, align_bytes=64, name="r_grouped")
+            for pair in range(n_tiles // 2):
+                piece = grouped[:, pair * 2 * P * PACK : (pair + 1) * 2 * P * PACK]
+                nc.scalar.copy(
+                    out=piece.bitcast(F32).rearrange("p (j u) -> p j u", u=2),
+                    in_=row_banks[n][pair][:].rearrange("p u j -> p j u"),
+                )
+            row_grouped[n] = grouped
+
+        def quantise_rows(n):
+            n_tiles, g, operand = row_units[n][1:4]
+            width = n_tiles * P
+            quantise(row_grouped[n][:, 0 : width * PACK], operand, g * width, width)
+
+        bias_count = BRANCHES * PASSES
         bias_bank = banks.tile([P, 2, 2 * P], F32, name="bank")
-        nc.tensor.transpose(bias_bank[:, 0, 0:P], bias_rows[:].bitcast(F32), identity[:])
-        bias_words = BRANCHES * rows_per_bias
-        bias_pairs = resident.tile([P, 2 * bias_words], BF16)
-        bias_t = resident.tile([P, 2 * bias_words], F32)
+        bias_pairs = resident.tile([P, bias_count * PACK], BF16)
+        bias_t = resident.tile([P, bias_count * PACK], F32)
+
+        def transpose_biases():
+            transpose_words(bias_bank, bias_rows, (0,), 0)
 
         def widen_biases():
-            nc.vector.tensor_copy(out=bias_pairs[:].bitcast(F32), in_=bias_bank[:, 0, 0:bias_words])
+            nc.vector.tensor_copy(
+                out=bias_pairs[:].bitcast(F32).rearrange("p (j u) -> p j u", u=2),
+                in_=bias_bank[:, :, 0:bias_count].rearrange("p u j -> p j u"),
+            )
             nc.vector.tensor_copy(out=bias_t[:], in_=bias_pairs[:])
 
         w_grouped = {}
@@ -167,18 +216,12 @@ def tile_executor_pa_kernel(
         def regroup_weights(unit):
             br, c, g = unit // UNITS_PER_BRANCH, (unit // PASSES) % PASSES, unit % PASSES
             grouped = w_stage.tile([P, K_PASS * PACK], BF16, align_bytes=64, name="w_grouped")
-            for u in range(2):
-                first = K_PASS * g + HALF_PASS * u
-                src = w_raw[(br, c)][:, :, first : first + HALF_PASS].rearrange(
-                    "p t (q e) -> p q t e", e=2
-                )
-                dst = grouped[:, u * HALF_PASS * PACK : (u + 1) * HALF_PASS * PACK].rearrange(
-                    "p (e q t) -> p q t e", e=2, t=PACK
-                )
-                if u == 0:
-                    nc.vector.tensor_copy(out=dst, in_=src)
-                else:
-                    nc.scalar.copy(out=dst, in_=src)
+            src = w_raw[(br, c)][:, :, K_PASS * g : K_PASS * (g + 1)].rearrange(
+                "p t (q i) -> p q t i", i=PACK
+            )
+            dst = grouped[:].rearrange("p (i q t) -> p q t i", i=PACK, t=PACK)
+            nc.vector.tensor_copy(out=dst[:, 0:VECTOR_SHARE], in_=src[:, 0:VECTOR_SHARE])
+            nc.scalar.copy(out=dst[:, VECTOR_SHARE:P], in_=src[:, VECTOR_SHARE:P])
             w_grouped[unit] = grouped
 
         def quantise_weights(unit):
@@ -207,72 +250,21 @@ def tile_executor_pa_kernel(
         def round_and_quantise_q(br, g):
             first = (br * PASSES + g) * PACK
             bias = bias_t[:, first : first + PACK].unsqueeze(1).to_broadcast([P, P, PACK])
-            rounded = []
+            q_grouped = q_stage.tile([P, BATCH_TILES, P, PACK], BF16, align_bytes=64)
             for h in range(BATCH_TILES):
-                q_grouped = q_stage.tile([P, P, PACK], BF16, align_bytes=64)
                 nc.vector.tensor_tensor(
-                    out=q_grouped[:],
+                    out=q_grouped[:, h],
                     in0=q_banks[(br, g, h)][:].rearrange("p t j -> p j t"),
                     in1=bias,
                     op=ADD,
                 )
-                rounded.append(q_grouped)
-            for h in range(BATCH_TILES):
-                quantise(
-                    rounded[h][:].rearrange("p j t -> p (j t)"),
-                    q_packed[br],
-                    g * BATCH + h * P,
-                    P,
-                )
-
-        pair_units = [(x_rows, 0, c, x_packed, c * BATCH) for c in range(PASSES)]
-        for br in range(BRANCHES):
-            for pair in range(KEY_TILES // 2):
-                for g in range(PASSES):
-                    pair_units.append(
-                        (key_rows[br], 2 * pair, g, k_packed[br], g * CODES + pair * 2 * P)
-                    )
-
-        def first_step(n):
-            if n < PASSES:
-                return X_FIRST_STEP + n
-            return KEY_FIRST_STEP + (n - PASSES) // KEY_UNITS_PER_STEP
-
-        def pair_units_begun_in(step):
-            return [n for n in range(len(pair_units)) if first_step(n) == step]
-
-        pair_banks = {}
-        pair_grouped = {}
-
-        def transpose_pairs(n):
-            rows, tile0, g = pair_units[n][0:3]
-            words = rows[:].bitcast(F32)
-            bank = banks.tile([P, 2, 2 * P], F32, name="bank")
-            for u in range(2):
-                for i in range(2):
-                    first = WORDS * (tile0 + i) + PASS_WORDS * g + P * u
-                    nc.tensor.transpose(
-                        bank[:, u, P * i : P * (i + 1)], words[:, first : first + P], identity[:]
-                    )
-            pair_banks[n] = bank
-
-        def interleave_pairs(n):
-            grouped = k_stage.tile([P, 2 * P * PACK], BF16, align_bytes=64, name="pair_grouped")
-            nc.scalar.copy(
-                out=grouped[:].bitcast(F32).rearrange("p (j u) -> p j u", u=2),
-                in_=pair_banks[n][:].rearrange("p u j -> p j u"),
-            )
-            pair_grouped[n] = grouped
-
-        def quantise_pairs(n):
-            operand, first = pair_units[n][3:5]
-            quantise(pair_grouped[n][:], operand, first, 2 * P)
+            quantise(q_grouped[:].rearrange("p h j t -> p (h j t)"), q_packed[br], g * BATCH, BATCH)
 
         def last_unit(br, g):
             return br * UNITS_PER_BRANCH + (PASSES - 1) * PASSES + g
 
         def score_step(br, g):
-            last_key_unit = PASSES + (br + 1) * KEY_UNITS - 1
+            last_key_unit = PASSES + (br + 1) * PASSES - 1
             return max(last_unit(br, g) + 2, first_step(last_key_unit) + 2)
 
         scores = {}
@@ -341,10 +333,12 @@ def tile_executor_pa_kernel(
                 for g in range(PASSES):
                     if step == last_unit(br, g) + 2:
                         round_and_quantise_q(br, g)
-            for n in pair_units_begun_in(step - 2):
-                quantise_pairs(n)
-            for n in pair_units_begun_in(step - 1):
-                interleave_pairs(n)
+            for n in row_units_begun_in(step - 2):
+                quantise_rows(n)
+            for n in row_units_begun_in(step - 1):
+                interleave_rows(n)
+            if step == X_FIRST_STEP - 1:
+                transpose_biases()
             for br in range(BRANCHES):
                 for g in range(PASSES):
                     if step == last_unit(br, g) + 1:
@@ -353,8 +347,8 @@ def tile_executor_pa_kernel(
                 for g in range(PASSES):
                     if step == score_step(br, g):
                         score_pass(br, g)
-            for n in pair_units_begun_in(step):
-                transpose_pairs(n)
+            for n in row_units_begun_in(step):
+                transpose_rows(n)
             for br in range(BRANCHES):
                 scored = score_step(br, PASSES - 1)
                 if step == scored + 1:

@@ -10,6 +10,8 @@ U32 = mybir.dt.uint32
 U8 = mybir.dt.uint8
 FP8X4 = mybir.dt.float8_e4m3fn_x4
 ADD = mybir.AluOpType.add
+MULT = mybir.AluOpType.mult
+MIN = mybir.AluOpType.min
 EXP = mybir.ActivationFunctionType.Exp
 COPY = mybir.ActivationFunctionType.Copy
 
@@ -33,7 +35,7 @@ UNITS_PER_BRANCH = PASSES * PASSES
 N_UNITS = BRANCHES * UNITS_PER_BRANCH
 X_FIRST_STEP = 3
 KEY_FIRST_STEP = 10
-VECTOR_SHARE = 64
+VECTOR_SHARE = 52
 
 
 def tile_executor_pa_kernel(
@@ -229,6 +231,7 @@ def tile_executor_pa_kernel(
             quantise(w_grouped[unit][:], w_packed[br], c * DIM + g * K_PASS, K_PASS)
 
         q_banks = {}
+        q_rounded = {}
 
         def project(br, g):
             for h in range(BATCH_TILES):
@@ -247,7 +250,7 @@ def tile_executor_pa_kernel(
                         )
                 q_banks[(br, g, h)] = bank
 
-        def round_and_quantise_q(br, g):
+        def round_q(br, g):
             first = (br * PASSES + g) * PACK
             bias = bias_t[:, first : first + PACK].unsqueeze(1).to_broadcast([P, P, PACK])
             q_grouped = q_stage.tile([P, BATCH_TILES, P, PACK], BF16, align_bytes=64)
@@ -258,14 +261,18 @@ def tile_executor_pa_kernel(
                     in1=bias,
                     op=ADD,
                 )
-            quantise(q_grouped[:].rearrange("p h j t -> p (h j t)"), q_packed[br], g * BATCH, BATCH)
+            q_rounded[(br, g)] = q_grouped
+
+        def quantise_q(br, g):
+            grouped = q_rounded[(br, g)][:].rearrange("p h j t -> p (h j t)")
+            quantise(grouped, q_packed[br], g * BATCH, BATCH)
 
         def last_unit(br, g):
             return br * UNITS_PER_BRANCH + (PASSES - 1) * PASSES + g
 
         def score_step(br, g):
             last_key_unit = PASSES + (br + 1) * PASSES - 1
-            return max(last_unit(br, g) + 2, first_step(last_key_unit) + 2)
+            return max(last_unit(br, g) + 3, first_step(last_key_unit) + 2)
 
         scores = {}
         shifts = {}
@@ -287,26 +294,30 @@ def tile_executor_pa_kernel(
                     stop=(g == PASSES - 1),
                 )
 
-        def row_maxima(br):
+        def scale_and_find_maxima(br):
+            probs[br] = resident.tile([P, BATCH_TILES, CODES], F32, name="probs_%d" % br)
             for h in range(BATCH_TILES):
-                row_max = small.tile([P, 1], F32)
-                nc.vector.reduce_max(
-                    out=row_max[:], in_=scores[(br, h)][:], axis=mybir.AxisListType.X
-                )
                 shift = small.tile([P, 1], F32)
-                nc.vector.tensor_scalar_mul(out=shift[:], in0=row_max[:], scalar1=-inv_sqrt_dim)
+                nc.vector.tensor_scalar(
+                    out=probs[br][:, h, :],
+                    in0=scores[(br, h)][:],
+                    scalar1=-inv_sqrt_dim,
+                    scalar2=None,
+                    op0=MULT,
+                    op1=MIN,
+                    accum_out=shift[:],
+                )
                 shifts[(br, h)] = shift
 
         def exponentials(br):
-            probs[br] = resident.tile([P, BATCH_TILES, CODES], F32, name="probs_%d" % br)
             for h in range(BATCH_TILES):
                 row_sum = small.tile([P, 1], F32)
                 nc.scalar.activation(
                     out=probs[br][:, h, :],
-                    in_=scores[(br, h)][:],
+                    in_=probs[br][:, h, :],
                     func=EXP,
                     bias=shifts[(br, h)][:],
-                    scale=inv_sqrt_dim,
+                    scale=-1.0,
                     accum_out=row_sum[:],
                 )
                 sums[(br, h)] = row_sum
@@ -325,6 +336,10 @@ def tile_executor_pa_kernel(
         for step in range(last_step + 1):
             if step < N_UNITS:
                 regroup_weights(step)
+            for br in range(BRANCHES):
+                for g in range(PASSES):
+                    if step == last_unit(br, g) + 3:
+                        quantise_q(br, g)
             if 0 <= step - 1 < N_UNITS:
                 quantise_weights(step - 1)
             if step == X_FIRST_STEP:
@@ -332,7 +347,7 @@ def tile_executor_pa_kernel(
             for br in range(BRANCHES):
                 for g in range(PASSES):
                     if step == last_unit(br, g) + 2:
-                        round_and_quantise_q(br, g)
+                        round_q(br, g)
             for n in row_units_begun_in(step - 2):
                 quantise_rows(n)
             for n in row_units_begun_in(step - 1):
@@ -352,7 +367,7 @@ def tile_executor_pa_kernel(
             for br in range(BRANCHES):
                 scored = score_step(br, PASSES - 1)
                 if step == scored + 1:
-                    row_maxima(br)
+                    scale_and_find_maxima(br)
                 if step == scored + 2:
                     exponentials(br)
                 if step == scored + 3:

@@ -34,8 +34,9 @@ FLOPS = BRANCHES * (2 * BATCH * DIM * DIM + 2 * BATCH * CODES * DIM)
 UNITS_PER_BRANCH = PASSES * PASSES
 N_UNITS = BRANCHES * UNITS_PER_BRANCH
 X_FIRST_STEP = 3
+BIAS_STEP = 6
 KEY_FIRST_STEP = 10
-VECTOR_SHARE = 52
+VECTOR_SHARE = 60
 
 
 def tile_executor_pa_kernel(
@@ -106,10 +107,10 @@ def tile_executor_pa_kernel(
             key_rows[br] = rows
 
         load_weights(0, 0)
-        load_biases()
         load_weights(0, 1)
         load_embedding()
         load_weights(0, 2)
+        load_biases()
         load_weights(1, 0)
         load_keys(0)
         load_weights(1, 1)
@@ -200,18 +201,16 @@ def tile_executor_pa_kernel(
 
         bias_count = BRANCHES * PASSES
         bias_bank = banks.tile([P, 2, 2 * P], F32, name="bank")
-        bias_pairs = resident.tile([P, bias_count * PACK], BF16)
-        bias_t = resident.tile([P, bias_count * PACK], F32)
+        bias_t = resident.tile([P, bias_count * PACK], BF16)
 
         def transpose_biases():
             transpose_words(bias_bank, bias_rows, (0,), 0)
 
-        def widen_biases():
+        def interleave_biases():
             nc.vector.tensor_copy(
-                out=bias_pairs[:].bitcast(F32).rearrange("p (j u) -> p j u", u=2),
+                out=bias_t[:].bitcast(F32).rearrange("p (j u) -> p j u", u=2),
                 in_=bias_bank[:, :, 0:bias_count].rearrange("p u j -> p j u"),
             )
-            nc.vector.tensor_copy(out=bias_t[:], in_=bias_pairs[:])
 
         w_grouped = {}
 
@@ -342,8 +341,8 @@ def tile_executor_pa_kernel(
                         quantise_q(br, g)
             if 0 <= step - 1 < N_UNITS:
                 quantise_weights(step - 1)
-            if step == X_FIRST_STEP:
-                widen_biases()
+            if step == BIAS_STEP + 1:
+                interleave_biases()
             for br in range(BRANCHES):
                 for g in range(PASSES):
                     if step == last_unit(br, g) + 2:
@@ -352,7 +351,7 @@ def tile_executor_pa_kernel(
                 quantise_rows(n)
             for n in row_units_begun_in(step - 1):
                 interleave_rows(n)
-            if step == X_FIRST_STEP - 1:
+            if step == BIAS_STEP:
                 transpose_biases()
             for br in range(BRANCHES):
                 for g in range(PASSES):
@@ -368,7 +367,7 @@ def tile_executor_pa_kernel(
                 scored = score_step(br, PASSES - 1)
                 if step == scored + 1:
                     scale_and_find_maxima(br)
-                if step == scored + 2:
+                if step == max(scored + 2, N_UNITS):
                     exponentials(br)
-                if step == scored + 3:
+                if step == max(scored + 2, N_UNITS) + 1:
                     normalise_and_store(br)

@@ -37,6 +37,8 @@ X_FIRST_STEP = 3
 BIAS_STEP = 6
 KEY_FIRST_STEP = 10
 VECTOR_SHARE = 60
+WARM_STEPS = 2
+WARM_PER_STEP = 2
 
 
 def tile_executor_pa_kernel(
@@ -56,7 +58,8 @@ def tile_executor_pa_kernel(
         r_stage = ctx.enter_context(tc.tile_pool(name="r_stage", bufs=3))
         q_stage = ctx.enter_context(tc.tile_pool(name="q_stage", bufs=2))
         small = ctx.enter_context(tc.tile_pool(name="small", bufs=4))
-        banks = ctx.enter_context(tc.psum_pool(name="banks", bufs=6))
+        banks = ctx.enter_context(tc.psum_pool(name="banks", bufs=5))
+        warm_psum = ctx.enter_context(tc.psum_pool(name="warm_psum", bufs=1))
         z_psum = ctx.enter_context(tc.psum_pool(name="z_psum", bufs=BATCH_TILES))
 
         identity = resident.tile([P, P], F32)
@@ -331,6 +334,14 @@ def tile_executor_pa_kernel(
                 )
                 nc.sync.dma_start(out=out_view[:, h, :], in_=probs[br][:, h, :])
 
+        warm_bank = warm_psum.tile([P, K_PASS], F32)
+
+        def warm_up(fresh):
+            for repeat in range(WARM_PER_STEP):
+                nc.tensor.matmul(
+                    out=warm_bank[:], lhsT=fresh[:, 0:P], rhs=fresh[:, 0:K_PASS], start=True, stop=True
+                )
+
         last_step = score_step(BRANCHES - 1, PASSES - 1) + 3
         for step in range(last_step + 1):
             if step < N_UNITS:
@@ -363,6 +374,9 @@ def tile_executor_pa_kernel(
                         score_pass(br, g)
             for n in row_units_begun_in(step):
                 transpose_rows(n)
+            for br in range(BRANCHES):
+                if last_unit(br, 0) - WARM_STEPS < step <= last_unit(br, 0):
+                    warm_up(w_grouped[step][:])
             for br in range(BRANCHES):
                 scored = score_step(br, PASSES - 1)
                 if step == scored + 1:

@@ -36,7 +36,7 @@ N_UNITS = BRANCHES * UNITS_PER_BRANCH
 X_FIRST_STEP = 3
 BIAS_STEP = 6
 KEY_FIRST_STEP = 10
-VECTOR_SHARE = 60
+VECTOR_SHARE = (64, 52)
 WARM_STEPS = 2
 WARM_PER_STEP = 2
 
@@ -224,8 +224,9 @@ def tile_executor_pa_kernel(
                 "p t (q i) -> p q t i", i=PACK
             )
             dst = grouped[:].rearrange("p (i q t) -> p q t i", i=PACK, t=PACK)
-            nc.vector.tensor_copy(out=dst[:, 0:VECTOR_SHARE], in_=src[:, 0:VECTOR_SHARE])
-            nc.scalar.copy(out=dst[:, VECTOR_SHARE:P], in_=src[:, VECTOR_SHARE:P])
+            share = VECTOR_SHARE[br]
+            nc.vector.tensor_copy(out=dst[:, 0:share], in_=src[:, 0:share])
+            nc.scalar.copy(out=dst[:, share:P], in_=src[:, share:P])
             w_grouped[unit] = grouped
 
         def quantise_weights(unit):
@@ -329,9 +330,18 @@ def tile_executor_pa_kernel(
             for h in range(BATCH_TILES):
                 inv_sum = small.tile([P, 1], F32)
                 nc.vector.reciprocal(out=inv_sum[:], in_=sums[(br, h)][:])
-                nc.scalar.activation(
-                    out=probs[br][:, h, :], in_=probs[br][:, h, :], func=COPY, scale=inv_sum[:]
-                )
+                if br == BRANCHES - 1:
+                    nc.vector.tensor_scalar(
+                        out=probs[br][:, h, :],
+                        in0=probs[br][:, h, :],
+                        scalar1=inv_sum[:],
+                        scalar2=None,
+                        op0=MULT,
+                    )
+                else:
+                    nc.scalar.activation(
+                        out=probs[br][:, h, :], in_=probs[br][:, h, :], func=COPY, scale=inv_sum[:]
+                    )
                 nc.sync.dma_start(out=out_view[:, h, :], in_=probs[br][:, h, :])
 
         warm_bank = warm_psum.tile([P, K_PASS], F32)

@@ -36,7 +36,7 @@ N_UNITS = BRANCHES * UNITS_PER_BRANCH
 X_FIRST_STEP = 3
 BIAS_STEP = 6
 KEY_FIRST_STEP = 10
-VECTOR_SHARE = (64, 52)
+VECTOR_SHARE = (68, 56)
 WARM_STEPS = 2
 WARM_PER_STEP = 2
 
@@ -267,8 +267,13 @@ def tile_executor_pa_kernel(
             q_rounded[(br, g)] = q_grouped
 
         def quantise_q(br, g):
-            grouped = q_rounded[(br, g)][:].rearrange("p h j t -> p (h j t)")
-            quantise(grouped, q_packed[br], g * BATCH, BATCH)
+            if (br, g) == (BRANCHES - 1, PASSES - 1):
+                for h in range(BATCH_TILES):
+                    grouped = q_rounded[(br, g)][:, h].rearrange("p j t -> p (j t)")
+                    quantise(grouped, q_packed[br], g * BATCH + h * P, P)
+            else:
+                grouped = q_rounded[(br, g)][:].rearrange("p h j t -> p (h j t)")
+                quantise(grouped, q_packed[br], g * BATCH, BATCH)
 
         def last_unit(br, g):
             return br * UNITS_PER_BRANCH + (PASSES - 1) * PASSES + g

@@ -221,12 +221,12 @@ def tile_executor_pa_kernel(
             br, c, g = unit // UNITS_PER_BRANCH, (unit // PASSES) % PASSES, unit % PASSES
             grouped = w_stage.tile([P, K_PASS * PACK], BF16, align_bytes=64, name="w_grouped")
             src = w_raw[(br, c)][:, :, K_PASS * g : K_PASS * (g + 1)].rearrange(
-                "p t (q i) -> p q t i", i=PACK
+                "p t (q d i) -> p q t d i", d=2, i=PACK
             )
-            dst = grouped[:].rearrange("p (i q t) -> p q t i", i=PACK, t=PACK)
-            share = VECTOR_SHARE[br]
+            dst = grouped[:].rearrange("p (i q d t) -> p q t d i", i=PACK, d=2, t=PACK)
+            share = VECTOR_SHARE[br] // 2
             nc.vector.tensor_copy(out=dst[:, 0:share], in_=src[:, 0:share])
-            nc.scalar.copy(out=dst[:, share:P], in_=src[:, share:P])
+            nc.scalar.copy(out=dst[:, share : P // 2], in_=src[:, share : P // 2])
             w_grouped[unit] = grouped
 
         def quantise_weights(unit):

from contextlib import ExitStack
import math

import concourse.mybir as mybir
from concourse.masks import make_identity

BF16 = mybir.dt.bfloat16
F32 = mybir.dt.float32
U32 = mybir.dt.uint32
U8 = mybir.dt.uint8
FP8X4 = mybir.dt.float8_e4m3fn_x4
ADD = mybir.AluOpType.add
MULT = mybir.AluOpType.mult
MIN = mybir.AluOpType.min
EXP = mybir.ActivationFunctionType.Exp
COPY = mybir.ActivationFunctionType.Copy

P = 128
PACK = 4
K_PASS = P * PACK
PASS_WORDS = K_PASS // 2

BATCH = 256
DIM = 1536
CODES = 512
PASSES = DIM // K_PASS
BATCH_TILES = BATCH // P
KEY_TILES = CODES // P
ROW_WORDS = DIM // 2
BRANCHES = 2

FLOPS = BRANCHES * (2 * BATCH * DIM * DIM + 2 * BATCH * CODES * DIM)

UNITS_PER_BRANCH = PASSES * PASSES
N_UNITS = BRANCHES * UNITS_PER_BRANCH
X_FIRST_STEP = 3
BIAS_STEP = 6
KEY_FIRST_STEP = 10
VECTOR_SHARE = (68, 56)
WARM_STEPS = 2
WARM_PER_STEP = 2


def tile_executor_pa_kernel(
    tc, inst_embed, Wfc, bfc, Wfp, bfp, Kc, Kp, out_0, out_1
):
    nc = tc.nc
    weights = (Wfc, Wfp)
    biases = (bfc, bfp)
    keys = (Kc, Kp)
    outs = (out_0, out_1)
    inv_sqrt_dim = 1.0 / math.sqrt(DIM)

    with ExitStack() as ctx:
        ctx.enter_context(tc.manual_schedule())
        resident = ctx.enter_context(tc.tile_pool(name="resident", bufs=1))
        w_stage = ctx.enter_context(tc.tile_pool(name="w_stage", bufs=6))
        r_stage = ctx.enter_context(tc.tile_pool(name="r_stage", bufs=3))
        q_stage = ctx.enter_context(tc.tile_pool(name="q_stage", bufs=2))
        small = ctx.enter_context(tc.tile_pool(name="small", bufs=4))
        banks = ctx.enter_context(tc.psum_pool(name="banks", bufs=5))
        warm_psum = ctx.enter_context(tc.psum_pool(name="warm_psum", bufs=1))
        z_psum = ctx.enter_context(tc.psum_pool(name="z_psum", bufs=BATCH_TILES))

        identity = resident.tile([P, P], F32)
        make_identity(nc, identity[:])

        exp_in = resident.tile([P, 1], F32)
        exp_out = resident.tile([P, 1], F32)
        nc.vector.memset(exp_in[:], 0.0)
        nc.scalar.activation(out=exp_out[:], in_=exp_in[:], func=EXP)

        bias_rows = resident.tile([P, K_PASS], BF16)
        nc.vector.memset(bias_rows[:], 0.0)

        w_raw = {}

        def load_weights(br, c):
            raw = resident.tile([P, PACK, DIM], BF16, name="w_raw_%d_%d" % (br, c))
            nc.sync.dma_start(
                out=raw[:],
                in_=weights[br][K_PASS * c : K_PASS * (c + 1), :].rearrange(
                    "(p t) n -> p t n", t=PACK
                ),
            )
            w_raw[(br, c)] = raw

        def load_biases():
            for br in range(BRANCHES):
                nc.sync.dma_start(
                    out=bias_rows[br * PASSES : (br + 1) * PASSES, :],
                    in_=biases[br].rearrange("(g k) -> g k", k=K_PASS),
                )

        x_rows = resident.tile([P, BATCH_TILES * DIM], BF16)

        def load_embedding():
            nc.sync.dma_start(
                out=x_rows[:], in_=inst_embed.rearrange("(p h) k -> p (h k)", h=BATCH_TILES)
            )

        key_rows = {}

        def load_keys(br):
            rows = resident.tile([P, KEY_TILES * DIM], BF16, name="key_rows_%d" % br)
            nc.sync.dma_start(
                out=rows[:].rearrange("p (r k) -> p r k", r=KEY_TILES),
                in_=keys[br].rearrange("(r p) k -> p r k", p=P),
            )
            key_rows[br] = rows

        load_weights(0, 0)
        load_weights(0, 1)
        load_embedding()
        load_weights(0, 2)
        load_biases()
        load_weights(1, 0)
        load_keys(0)
        load_weights(1, 1)
        load_keys(1)
        load_weights(1, 2)

        def packed(name, width):
            codes = resident.tile([P, width], U32, align_bytes=64, name="%s_codes" % name)
            scales = resident.tile([P, width], U8, align_bytes=64, name="%s_scales" % name)
            return codes, scales

        x_packed = packed("x", PASSES * BATCH)
        w_packed = [packed("w%d" % br, PASSES * DIM) for br in range(BRANCHES)]
        q_packed = [packed("q%d" % br, PASSES * BATCH) for br in range(BRANCHES)]
        k_packed = [packed("k%d" % br, PASSES * CODES) for br in range(BRANCHES)]

        def quantise(grouped, operand, first, width):
            codes, scales = operand
            nc.vector.quantize_mx(
                out=codes[:, first : first + width].bitcast(FP8X4),
                scales=scales[:, first : first + width],
                in_=grouped,
            )

        def multiply(out, stationary, s_first, moving, m_first, m_width, start, stop):
            s_codes, s_scales = stationary
            m_codes, m_scales = moving
            nc.tensor.matmul_mx(
                out=out,
                lhsT=s_codes[:, s_first : s_first + P].bitcast(FP8X4),
                lhsT_scale=s_scales[:, s_first : s_first + P],
                rhs=m_codes[:, m_first : m_first + m_width].bitcast(FP8X4),
                rhs_scale=m_scales[:, m_first : m_first + m_width],
                start=start,
                stop=stop,
            )

        def transpose_words(bank, rows, tiles, g):
            words = rows[:].bitcast(F32)
            for u in range(2):
                for i in range(len(tiles)):
                    first = ROW_WORDS * tiles[i] + PASS_WORDS * g
                    nc.tensor.transpose(
                        bank[:, u, P * i : P * (i + 1)],
                        words[:, first + u : first + PASS_WORDS : 2],
                        identity[:],
                    )

        row_units = [(x_rows, BATCH_TILES, c, x_packed) for c in range(PASSES)]
        for br in range(BRANCHES):
            for g in range(PASSES):
                row_units.append((key_rows[br], KEY_TILES, g, k_packed[br]))

        def first_step(n):
            if n < PASSES:
                return X_FIRST_STEP + n
            return KEY_FIRST_STEP + n - PASSES

        def row_units_begun_in(step):
            return [n for n in range(len(row_units)) if first_step(n) == step]

        row_banks = {}
        row_grouped = {}

        def transpose_rows(n):
            rows, n_tiles, g = row_units[n][0:3]
            row_banks[n] = []
            for pair in range(n_tiles // 2):
                bank = banks.tile([P, 2, 2 * P], F32, name="bank")
                transpose_words(bank, rows, (2 * pair, 2 * pair + 1), g)
                row_banks[n].append(bank)

        def interleave_rows(n):
            n_tiles = row_units[n][1]
            grouped = r_stage.tile([P, KEY_TILES * P * PACK], BF16, align_bytes=64, name="r_grouped")
            for pair in range(n_tiles // 2):
                piece = grouped[:, pair * 2 * P * PACK : (pair + 1) * 2 * P * PACK]
                nc.scalar.copy(
                    out=piece.bitcast(F32).rearrange("p (j u) -> p j u", u=2),
                    in_=row_banks[n][pair][:].rearrange("p u j -> p j u"),
                )
            row_grouped[n] = grouped

        def quantise_rows(n):
            n_tiles, g, operand = row_units[n][1:4]
            width = n_tiles * P
            quantise(row_grouped[n][:, 0 : width * PACK], operand, g * width, width)

        bias_count = BRANCHES * PASSES
        bias_bank = banks.tile([P, 2, 2 * P], F32, name="bank")
        bias_t = resident.tile([P, bias_count * PACK], BF16)

        def transpose_biases():
            transpose_words(bias_bank, bias_rows, (0,), 0)

        def interleave_biases():
            nc.vector.tensor_copy(
                out=bias_t[:].bitcast(F32).rearrange("p (j u) -> p j u", u=2),
                in_=bias_bank[:, :, 0:bias_count].rearrange("p u j -> p j u"),
            )

        w_grouped = {}

        def regroup_weights(unit):
            br, c, g = unit // UNITS_PER_BRANCH, (unit // PASSES) % PASSES, unit % PASSES
            grouped = w_stage.tile([P, K_PASS * PACK], BF16, align_bytes=64, name="w_grouped")
            src = w_raw[(br, c)][:, :, K_PASS * g : K_PASS * (g + 1)].rearrange(
                "p t (q d i) -> p q t d i", d=2, i=PACK
            )
            dst = grouped[:].rearrange("p (i q d t) -> p q t d i", i=PACK, d=2, t=PACK)
            share = VECTOR_SHARE[br] // 2
            nc.vector.tensor_copy(out=dst[:, 0:share], in_=src[:, 0:share])
            nc.scalar.copy(out=dst[:, share : P // 2], in_=src[:, share : P // 2])
            w_grouped[unit] = grouped

        def quantise_weights(unit):
            br, c, g = unit // UNITS_PER_BRANCH, (unit // PASSES) % PASSES, unit % PASSES
            quantise(w_grouped[unit][:], w_packed[br], c * DIM + g * K_PASS, K_PASS)

        q_banks = {}
        q_rounded = {}

        def project(br, g):
            for h in range(BATCH_TILES):
                bank = banks.tile([P, PACK, P], F32, name="bank")
                for t in range(PACK):
                    for c in range(PASSES):
                        multiply(
                            bank[:, t, :],
                            w_packed[br],
                            c * DIM + g * K_PASS + t * P,
                            x_packed,
                            c * BATCH + h * P,
                            P,
                            start=(c == 0),
                            stop=(c == PASSES - 1),
                        )
                q_banks[(br, g, h)] = bank

        def round_q(br, g):
            first = (br * PASSES + g) * PACK
            bias = bias_t[:, first : first + PACK].unsqueeze(1).to_broadcast([P, P, PACK])
            q_grouped = q_stage.tile([P, BATCH_TILES, P, PACK], BF16, align_bytes=64)
            for h in range(BATCH_TILES):
                nc.vector.tensor_tensor(
                    out=q_grouped[:, h],
                    in0=q_banks[(br, g, h)][:].rearrange("p t j -> p j t"),
                    in1=bias,
                    op=ADD,
                )
            q_rounded[(br, g)] = q_grouped

        def quantise_q(br, g):
            if (br, g) == (BRANCHES - 1, PASSES - 1):
                for h in range(BATCH_TILES):
                    grouped = q_rounded[(br, g)][:, h].rearrange("p j t -> p (j t)")
                    quantise(grouped, q_packed[br], g * BATCH + h * P, P)
            else:
                grouped = q_rounded[(br, g)][:].rearrange("p h j t -> p (h j t)")
                quantise(grouped, q_packed[br], g * BATCH, BATCH)

        def last_unit(br, g):
            return br * UNITS_PER_BRANCH + (PASSES - 1) * PASSES + g

        def score_step(br, g):
            last_key_unit = PASSES + (br + 1) * PASSES - 1
            return max(last_unit(br, g) + 3, first_step(last_key_unit) + 2)

        scores = {}
        shifts = {}
        sums = {}
        probs = {}

        def score_pass(br, g):
            for h in range(BATCH_TILES):
                if g == 0:
                    scores[(br, h)] = z_psum.tile([P, CODES], F32, name="scores")
                multiply(
                    scores[(br, h)][:],
                    q_packed[br],
                    g * BATCH + h * P,
                    k_packed[br],
                    g * CODES,
                    CODES,
                    start=(g == 0),
                    stop=(g == PASSES - 1),
                )

        def scale_and_find_maxima(br):
            probs[br] = resident.tile([P, BATCH_TILES, CODES], F32, name="probs_%d" % br)
            for h in range(BATCH_TILES):
                shift = small.tile([P, 1], F32)
                nc.vector.tensor_scalar(
                    out=probs[br][:, h, :],
                    in0=scores[(br, h)][:],
                    scalar1=-inv_sqrt_dim,
                    scalar2=None,
                    op0=MULT,
                    op1=MIN,
                    accum_out=shift[:],
                )
                shifts[(br, h)] = shift

        def exponentials(br):
            for h in range(BATCH_TILES):
                row_sum = small.tile([P, 1], F32)
                nc.scalar.activation(
                    out=probs[br][:, h, :],
                    in_=probs[br][:, h, :],
                    func=EXP,
                    bias=shifts[(br, h)][:],
                    scale=-1.0,
                    accum_out=row_sum[:],
                )
                sums[(br, h)] = row_sum

        def normalise_and_store(br):
            out_view = outs[br].rearrange("(p h) n -> p h n", h=BATCH_TILES)
            for h in range(BATCH_TILES):
                inv_sum = small.tile([P, 1], F32)
                nc.vector.reciprocal(out=inv_sum[:], in_=sums[(br, h)][:])
                if br == BRANCHES - 1:
                    nc.vector.tensor_scalar(
                        out=probs[br][:, h, :],
                        in0=probs[br][:, h, :],
                        scalar1=inv_sum[:],
                        scalar2=None,
                        op0=MULT,
                    )
                else:
                    nc.scalar.activation(
                        out=probs[br][:, h, :], in_=probs[br][:, h, :], func=COPY, scale=inv_sum[:]
                    )
                nc.sync.dma_start(out=out_view[:, h, :], in_=probs[br][:, h, :])

        warm_bank = warm_psum.tile([P, K_PASS], F32)

        def warm_up(fresh):
            for repeat in range(WARM_PER_STEP):
                nc.tensor.matmul(
                    out=warm_bank[:], lhsT=fresh[:, 0:P], rhs=fresh[:, 0:K_PASS], start=True, stop=True
                )

        last_step = score_step(BRANCHES - 1, PASSES - 1) + 3
        for step in range(last_step + 1):
            if step < N_UNITS:
                regroup_weights(step)
            for br in range(BRANCHES):
                for g in range(PASSES):
                    if step == last_unit(br, g) + 3:
                        quantise_q(br, g)
            if 0 <= step - 1 < N_UNITS:
                quantise_weights(step - 1)
            if step == BIAS_STEP + 1:
                interleave_biases()
            for br in range(BRANCHES):
                for g in range(PASSES):
                    if step == last_unit(br, g) + 2:
                        round_q(br, g)
            for n in row_units_begun_in(step - 2):
                quantise_rows(n)
            for n in row_units_begun_in(step - 1):
                interleave_rows(n)
            if step == BIAS_STEP:
                transpose_biases()
            for br in range(BRANCHES):
                for g in range(PASSES):
                    if step == last_unit(br, g) + 1:
                        project(br, g)
            for br in range(BRANCHES):
                for g in range(PASSES):
                    if step == score_step(br, g):
                        score_pass(br, g)
            for n in row_units_begun_in(step):
                transpose_rows(n)
            for br in range(BRANCHES):
                if last_unit(br, 0) - WARM_STEPS < step <= last_unit(br, 0):
                    warm_up(w_grouped[step][:])
            for br in range(BRANCHES):
                scored = score_step(br, PASSES - 1)
                if step == scored + 1:
                    scale_and_find_maxima(br)
                if step == max(scored + 2, N_UNITS):
                    exponentials(br)
                if step == max(scored + 2, N_UNITS) + 1:
                    normalise_and_store(br)
